import numpy as np
import ml_dtypes


def mxq(x, axis, fmt="e4m3"):
    dtype, down = {"e4m3": (ml_dtypes.float8_e4m3fn, 7), "e5m2": (ml_dtypes.float8_e5m2, 14)}[fmt]
    v = np.moveaxis(np.asarray(x, np.float32).astype(ml_dtypes.bfloat16).astype(np.float64), axis, -1)
    blocks = v.reshape(v.shape[:-1] + (-1, 32))
    amax = np.abs(blocks).max(-1, keepdims=True)
    byte = np.maximum(np.where(amax > 0, np.frexp(amax)[1] - 1 + 127, 0) - down, 1)
    scale = np.exp2(byte - 127.0)
    codes = (blocks / scale).astype(np.float32).astype(dtype).astype(np.float64)
    return np.moveaxis((codes * scale).reshape(v.shape), -1, axis)


WIDE = False


def mx_kscale(k):
    if not WIDE:
        return np.ones(k)
    levels = np.array([10, -10, 5, -5, 0])
    a = np.random.permutation(np.resize(levels, k // 512 * 4)).reshape(k // 512, 4)
    idx = np.arange(k)
    return np.exp2(a[idx // 512, idx % 128 // 32])


BF16 = ml_dtypes.bfloat16


def bf(x):
    return np.asarray(x, np.float32).astype(BF16)


def f64(x):
    return np.asarray(x).astype(np.float64)


B, S, K, N = 2, 512, 2048, 2048
FP8_MAX = 448.0
EPS = 1e-12


def setup_inputs():
    s = mx_kscale(K)
    return {"x": bf(np.random.standard_normal((B, S, K)) * s),
            "weight": bf(np.random.standard_normal((K, N)) * 1.28 / np.sqrt(K) / s[:, None])}


def reference(x, weight):
    x = f64(x)
    weight = f64(weight)
    b, sl, k = x.shape
    n = weight.shape[1]
    x2 = x.reshape(-1, k)
    x_scale = FP8_MAX / np.maximum(np.max(np.abs(x2)), EPS)
    w_scale = FP8_MAX / np.maximum(np.max(np.abs(weight)), EPS)
    x_sim = np.clip(x2 * x_scale, -FP8_MAX, FP8_MAX)
    w_sim = np.clip(weight * w_scale, -FP8_MAX, FP8_MAX)
    out = (mxq(x_sim, 1, "e4m3") @ mxq(w_sim, 0, "e4m3")) * (1.0 / (x_scale * w_scale))
    return out.reshape(b, sl, n)

@@ -1,0 +1,192 @@
+from contextlib import ExitStack
+
+import concourse.mybir as mybir
+from concourse.masks import make_identity
+
+BF16 = mybir.dt.bfloat16
+F32 = mybir.dt.float32
+I32 = mybir.dt.int32
+U32 = mybir.dt.uint32
+U8 = mybir.dt.uint8
+FP8X4 = mybir.dt.float8_e4m3fn_x4
+ALU = mybir.AluOpType
+ACTF = mybir.ActivationFunctionType
+AX = mybir.AxisListType
+
+P = 128
+M, K, N = 1024, 2048, 2048
+MT = M // P
+G = K // 512
+NW = 512
+NJ = N // NW
+FP8_MAX = 448.0
+EPS = 1e-12
+ABS_MASK = 0x7FFF7FFF
+
+FLOPS = 2 * M * K * N
+
+X_ABS = ["V", "V", "A", "V", "A", "V", "A", "V"]
+W_ABS = ["A", "V", "V", "V", "V", "V", "V", "V"]
+W_REG = [["V", "A", "V", "A"], ["V", "V", "V", "A"], ["V", "V", "V", "A"], ["V", "V", "V", "A"]]
+
+
+def tile_modelnew_kernel(tc, x, weight, out):
+    nc = tc.nc
+    xv = x.flatten_outer_dims().rearrange("(p i) k -> p i k", i=MT)
+    ov = out.flatten_outer_dims().rearrange("(p i) n -> p i n", i=MT)
+    wv = weight.rearrange("(c p e) n -> p c (e n)", p=P, e=2)
+
+    with ExitStack() as ctx:
+        keep = ctx.enter_context(tc.tile_pool(name="keep", bufs=1))
+        t4k = ctx.enter_context(tc.tile_pool(name="t4k", bufs=8))
+        scr = ctx.enter_context(tc.tile_pool(name="scr", bufs=3))
+        ostp = ctx.enter_context(tc.tile_pool(name="ostp", bufs=6))
+
+        w_raw = keep.tile([P, 2 * G, 2 * N], BF16)
+        xga = keep.tile([P, G, MT, 4 * P], BF16, align_bytes=64)
+        xc = keep.tile([P, G * MT * P], U32, align_bytes=64)
+        xp = keep.tile([P, G * MT * P], U8, align_bytes=64)
+        wc = keep.tile([P, NJ * G * NW], U32, align_bytes=64)
+        wp = keep.tile([P, NJ * G * NW], U8, align_bytes=64)
+        ident = keep.tile([P, P], F32)
+        xcols = keep.tile([P, 4], F32)
+        wcols = keep.tile([P, 8], F32)
+        xm = keep.tile([P, 1], F32)
+        wm = keep.tile([P, 1], F32)
+        xgm = keep.tile([P, 1], F32)
+        wgm = keep.tile([P, 1], F32)
+        xr = keep.tile([P, 1], F32)
+        wr = keep.tile([P, 1], F32)
+        xs = keep.tile([P, 1], F32)
+        ws = keep.tile([P, 1], F32)
+        inv = keep.tile([P, 1], F32)
+
+        make_identity(nc, ident[:])
+
+        x_raw = []
+        for i in range(MT):
+            xt_i = t4k.tile([P, K], BF16, name="xraw%d" % i, tag="t4k", align_bytes=64)
+            nc.sync.dma_start(out=xt_i[:], in_=xv[:, i, :])
+            x_raw.append(xt_i)
+        for c in range(2 * G):
+            nc.sync.dma_start(out=w_raw[:, c, :], in_=wv[:, c, :])
+
+        def take_abs(dst, src, how):
+            if how == "V":
+                nc.vector.tensor_scalar(out=dst.bitcast(I32), in0=src.bitcast(I32),
+                                        scalar1=ABS_MASK, scalar2=None, op0=ALU.bitwise_and)
+            else:
+                nc.scalar.activation(out=dst, in_=src, func=ACTF.Abs)
+
+        def take_max(s, col):
+            nc.vector.tensor_scalar(out=s[:], in0=s[:], scalar1=1.0, scalar2=None,
+                                    op0=ALU.mult, op1=ALU.max, accum_out=col)
+
+        def quantise_x(g):
+            nc.vector.quantize_mx(out=xc[:, g * MT * P:(g + 1) * MT * P].bitcast(FP8X4),
+                                  scales=xp[:, g * MT * P:(g + 1) * MT * P],
+                                  in_=xga[:, g].rearrange("p i c -> p (i c)"))
+
+        with tc.psum_pool(name="psa", bufs=6) as psa:
+            for q in range(MT // 2):
+                s = scr.tile([P, 2 * K], BF16, name="s", tag="s")
+                take_abs(s[:, 0:K], x_raw[2 * q][:], X_ABS[2 * q])
+                take_abs(s[:, K:2 * K], x_raw[2 * q + 1][:], X_ABS[2 * q + 1])
+                take_max(s, xcols[:, q:q + 1])
+            nc.vector.tensor_reduce(out=xm[:], in_=xcols[:], axis=AX.X, op=ALU.max)
+            bcx = psa.tile([P, P], F32, name="bcx", tag="bc", bufs=1)
+            nc.tensor.matmul(out=bcx[:], lhsT=xm[:, 0:1].to_broadcast([P, P]), rhs=ident[:],
+                             start=True, stop=True)
+            nc.vector.tensor_reduce(out=xgm[:], in_=bcx[:], axis=AX.X, op=ALU.max)
+            nc.vector.tensor_scalar(out=xr[:], in0=xgm[:], scalar1=EPS, scalar2=1.0 / FP8_MAX,
+                                    op0=ALU.max, op1=ALU.mult)
+            nc.vector.reciprocal(out=xs[:], in_=xr[:])
+
+            for h in range(2):
+                for i in range(MT):
+                    xw = x_raw[i][:].bitcast(F32)
+                    xt = psa.tile([P, 2, 2, P], F32, name="xt", tag="xt")
+                    for gg in range(2):
+                        for u in range(2):
+                            w0 = 256 * (2 * h + gg) + 128 * u
+                            nc.tensor.transpose(xt[:, u, gg, :], xw[:, w0:w0 + P], ident[:])
+                    nc.scalar.activation(
+                        out=xga[:, 2 * h:2 * h + 2, i, :].rearrange("p g (r u e) -> p g r u e", u=2, e=2),
+                        in_=xt[:].bitcast(BF16).rearrange("p u g (r e) -> p g r u e", e=2),
+                        func=ACTF.Copy, scale=xs[:, 0:1])
+
+            for c in range(2 * G):
+                s = scr.tile([P, 2 * K], BF16, name="s", tag="s")
+                take_abs(s[:], w_raw[:, c, :], W_ABS[c])
+                take_max(s, wcols[:, c:c + 1])
+            nc.vector.tensor_reduce(out=wm[:], in_=wcols[:], axis=AX.X, op=ALU.max)
+            bcw = psa.tile([P, P], F32, name="bcw", tag="bc", bufs=1)
+            nc.tensor.matmul(out=bcw[:], lhsT=wm[:, 0:1].to_broadcast([P, P]), rhs=ident[:],
+                             start=True, stop=True)
+            quantise_x(0)
+            nc.vector.tensor_reduce(out=wgm[:], in_=bcw[:], axis=AX.X, op=ALU.max)
+            nc.vector.tensor_scalar(out=wr[:], in0=wgm[:], scalar1=EPS, scalar2=1.0 / FP8_MAX,
+                                    op0=ALU.max, op1=ALU.mult)
+            nc.vector.reciprocal(out=ws[:], in_=wr[:])
+
+        w4 = w_raw[:].rearrange("p c (e n) -> p (c e) n", e=2)
+
+        def regroup_w(j, g):
+            wg = t4k.tile([P, 4 * NW], BF16, name="wg", tag="t4k", align_bytes=64)
+            src = w4[:, 4 * g:4 * g + 4, j * NW:(j + 1) * NW].rearrange("p t (c i) -> p c t i", i=4)
+            dst = wg[:].rearrange("p (c i t) -> p c t i", i=4, t=4)
+            if W_REG[j][g] == "V":
+                nc.vector.tensor_scalar(out=dst, in0=src, scalar1=ws[:, 0:1], scalar2=None,
+                                        op0=ALU.mult)
+            else:
+                nc.scalar.activation(out=dst, in_=src, func=ACTF.Copy, scale=ws[:, 0:1])
+            return wg
+
+        def quantise_w(j, g, wg):
+            b = (j * G + g) * NW
+            nc.vector.quantize_mx(out=wc[:, b:b + NW].bitcast(FP8X4), scales=wp[:, b:b + NW],
+                                  in_=wg[:])
+
+        def mx_pass(acc, i, j, g):
+            a = (g * MT + i) * P
+            b = (j * G + g) * NW
+            nc.tensor.matmul_mx(out=acc[:], lhsT=xc[:, a:a + P].bitcast(FP8X4), lhsT_scale=xp[:, a:a + P],
+                                rhs=wc[:, b:b + NW].bitcast(FP8X4), rhs_scale=wp[:, b:b + NW],
+                                start=(g == 0), stop=(g == G - 1))
+
+        def finish(acc, i, j):
+            o = ostp.tile([P, NW], F32, name="o", tag="o")
+            if i % 4 == 3:
+                nc.vector.tensor_scalar(out=o[:], in0=acc[:], scalar1=inv[:, 0:1], scalar2=None,
+                                        op0=ALU.mult)
+            else:
+                nc.scalar.activation(out=o[:], in_=acc[:], func=ACTF.Copy, scale=inv[:, 0:1])
+            nc.sync.dma_start(out=ov[:, i, j * NW:(j + 1) * NW], in_=o[:])
+
+        with tc.psum_pool(name="psb", bufs=8) as psb:
+            accs = []
+            for i in range(MT):
+                acc0 = psb.tile([P, NW], F32, name="acc", tag="acc")
+                accs.append(acc0)
+            for g in range(G):
+                wg = regroup_w(0, g)
+                if g > 0:
+                    quantise_x(g)
+                quantise_w(0, g, wg)
+                for i in range(MT):
+                    mx_pass(accs[i], i, 0, g)
+            nc.vector.tensor_tensor(out=inv[:], in0=xr[:], in1=wr[:], op=ALU.mult)
+            for j in range(1, NJ):
+                wgs = []
+                for g in range(G):
+                    wgs.append(regroup_w(j, g))
+                for g in range(G):
+                    quantise_w(j, g, wgs[g])
+                if j == 1:
+                    for i in range(MT):
+                        finish(accs[i], i, 0)
+                for i in range(MT):
+                    acc = psb.tile([P, NW], F32, name="acc", tag="acc")
+                    for g in range(G):
+                        mx_pass(acc, i, j, g)
+                    finish(acc, i, j)

@@ -22,12 +22,10 @@ NJ = N // NW
 FP8_MAX = 448.0
 EPS = 1e-12
 ABS_MASK = 0x7FFF7FFF
+XT_BANKS = 7
+DUMMIES = 0
 
 FLOPS = 2 * M * K * N
-
-X_ABS = ["V", "V", "A", "V", "A", "V", "A", "V"]
-W_ABS = ["A", "V", "V", "V", "V", "V", "V", "V"]
-W_REG = [["V", "A", "V", "A"], ["V", "V", "V", "A"], ["V", "V", "V", "A"], ["V", "V", "V", "A"]]
 
 
 def tile_modelnew_kernel(tc, x, weight, out):
@@ -41,6 +39,7 @@ def tile_modelnew_kernel(tc, x, weight, out):
         t4k = ctx.enter_context(tc.tile_pool(name="t4k", bufs=8))
         scr = ctx.enter_context(tc.tile_pool(name="scr", bufs=3))
         ostp = ctx.enter_context(tc.tile_pool(name="ostp", bufs=6))
+        ctx.enter_context(tc.manual_schedule())
 
         w_raw = keep.tile([P, 2 * G, 2 * N], BF16)
         xga = keep.tile([P, G, MT, 4 * P], BF16, align_bytes=64)
@@ -49,12 +48,8 @@ def tile_modelnew_kernel(tc, x, weight, out):
         wc = keep.tile([P, NJ * G * NW], U32, align_bytes=64)
         wp = keep.tile([P, NJ * G * NW], U8, align_bytes=64)
         ident = keep.tile([P, P], F32)
-        xcols = keep.tile([P, 4], F32)
-        wcols = keep.tile([P, 8], F32)
-        xm = keep.tile([P, 1], F32)
-        wm = keep.tile([P, 1], F32)
-        xgm = keep.tile([P, 1], F32)
-        wgm = keep.tile([P, 1], F32)
+        idsc = keep.tile([P, P], F32)
+        cols = keep.tile([P, 12], F32)
         xr = keep.tile([P, 1], F32)
         wr = keep.tile([P, 1], F32)
         xs = keep.tile([P, 1], F32)
@@ -62,90 +57,141 @@ def tile_modelnew_kernel(tc, x, weight, out):
         inv = keep.tile([P, 1], F32)
 
         make_identity(nc, ident[:])
+        nc.vector.tensor_scalar(out=idsc[:], in0=ident[:], scalar1=1.0 / FP8_MAX, scalar2=None,
+                                op0=ALU.mult)
 
         x_raw = []
         for i in range(MT):
             xt_i = t4k.tile([P, K], BF16, name="xraw%d" % i, tag="t4k", align_bytes=64)
-            nc.sync.dma_start(out=xt_i[:], in_=xv[:, i, :])
+            if i == 0:
+                nc.sync.dma_start(out=xt_i[:, 0:K // 2], in_=xv[:, i, 0:K // 2])
+                nc.sync.dma_start(out=xt_i[:, K // 2:K], in_=xv[:, i, K // 2:K])
+            else:
+                nc.sync.dma_start(out=xt_i[:], in_=xv[:, i, :])
             x_raw.append(xt_i)
         for c in range(2 * G):
             nc.sync.dma_start(out=w_raw[:, c, :], in_=wv[:, c, :])
 
-        def take_abs(dst, src, how):
-            if how == "V":
+        groups = {}
+
+        def unit_src(k, lo, hi):
+            if k >= 4:
+                return w_raw[:, k - 4, lo:hi]
+            return x_raw[2 * k + lo // K][:, lo % K:(hi - 1) % K + 1]
+
+        def take_abs(k, lo, hi, eng):
+            if k not in groups:
+                s_new = scr.tile([P, 2 * K], BF16, name="s", tag="s")
+                groups[k] = s_new
+            dst = groups[k][:, lo:hi]
+            src = unit_src(k, lo, hi)
+            if eng == "V":
                 nc.vector.tensor_scalar(out=dst.bitcast(I32), in0=src.bitcast(I32),
                                         scalar1=ABS_MASK, scalar2=None, op0=ALU.bitwise_and)
             else:
                 nc.scalar.activation(out=dst, in_=src, func=ACTF.Abs)
 
-        def take_max(s, col):
-            nc.vector.tensor_scalar(out=s[:], in0=s[:], scalar1=1.0, scalar2=None,
-                                    op0=ALU.mult, op1=ALU.max, accum_out=col)
+        def take_max(k):
+            s = groups[k]
+            start = EPS if k in (0, 4) else cols[:, k - 1:k]
+            nc.vector.tensor_scalar(out=s[:], in0=s[:], scalar1=1.0, scalar2=start,
+                                    op0=ALU.mult, op1=ALU.max, accum_out=cols[:, k:k + 1])
 
         def quantise_x(g):
             nc.vector.quantize_mx(out=xc[:, g * MT * P:(g + 1) * MT * P].bitcast(FP8X4),
                                   scales=xp[:, g * MT * P:(g + 1) * MT * P],
                                   in_=xga[:, g].rearrange("p i c -> p (i c)"))
 
-        with tc.psum_pool(name="psa", bufs=6) as psa:
-            for q in range(MT // 2):
-                s = scr.tile([P, 2 * K], BF16, name="s", tag="s")
-                take_abs(s[:, 0:K], x_raw[2 * q][:], X_ABS[2 * q])
-                take_abs(s[:, K:2 * K], x_raw[2 * q + 1][:], X_ABS[2 * q + 1])
-                take_max(s, xcols[:, q:q + 1])
-            nc.vector.tensor_reduce(out=xm[:], in_=xcols[:], axis=AX.X, op=ALU.max)
-            bcx = psa.tile([P, P], F32, name="bcx", tag="bc", bufs=1)
-            nc.tensor.matmul(out=bcx[:], lhsT=xm[:, 0:1].to_broadcast([P, P]), rhs=ident[:],
-                             start=True, stop=True)
-            nc.vector.tensor_reduce(out=xgm[:], in_=bcx[:], axis=AX.X, op=ALU.max)
-            nc.vector.tensor_scalar(out=xr[:], in0=xgm[:], scalar1=EPS, scalar2=1.0 / FP8_MAX,
-                                    op0=ALU.max, op1=ALU.mult)
-            nc.vector.reciprocal(out=xs[:], in_=xr[:])
+        with tc.psum_pool(name="psa", bufs=XT_BANKS) as psa:
+            banks = {}
 
-            for h in range(2):
-                for i in range(MT):
-                    xw = x_raw[i][:].bitcast(F32)
-                    xt = psa.tile([P, 2, 2, P], F32, name="xt", tag="xt")
-                    for gg in range(2):
-                        for u in range(2):
-                            w0 = 256 * (2 * h + gg) + 128 * u
-                            nc.tensor.transpose(xt[:, u, gg, :], xw[:, w0:w0 + P], ident[:])
-                    nc.scalar.activation(
-                        out=xga[:, 2 * h:2 * h + 2, i, :].rearrange("p g (r u e) -> p g r u e", u=2, e=2),
-                        in_=xt[:].bitcast(BF16).rearrange("p u g (r e) -> p g r u e", e=2),
-                        func=ACTF.Copy, scale=xs[:, 0:1])
+            def transposes(n):
+                h, i = n // MT, n % MT
+                xw = x_raw[i][:].bitcast(F32)
+                xt = psa.tile([P, 2, 2, P], F32, name="xt", tag="xt")
+                for gg in range(2):
+                    for u in range(2):
+                        w0 = 256 * (2 * h + gg) + 128 * u
+                        nc.tensor.transpose(xt[:, u, gg, :], xw[:, w0:w0 + P], ident[:])
+                banks[n] = xt
 
-            for c in range(2 * G):
-                s = scr.tile([P, 2 * K], BF16, name="s", tag="s")
-                take_abs(s[:], w_raw[:, c, :], W_ABS[c])
-                take_max(s, wcols[:, c:c + 1])
-            nc.vector.tensor_reduce(out=wm[:], in_=wcols[:], axis=AX.X, op=ALU.max)
-            bcw = psa.tile([P, P], F32, name="bcw", tag="bc", bufs=1)
-            nc.tensor.matmul(out=bcw[:], lhsT=wm[:, 0:1].to_broadcast([P, P]), rhs=ident[:],
-                             start=True, stop=True)
+            def evict_x(n):
+                h, i = n // MT, n % MT
+                nc.scalar.activation(
+                    out=xga[:, 2 * h:2 * h + 2, i, :].rearrange("p g (r u e) -> p g r u e", u=2, e=2),
+                    in_=banks[n][:].bitcast(BF16).rearrange("p u g (r e) -> p g r u e", e=2),
+                    func=ACTF.Copy, scale=xs[:, 0:1])
+                if n + XT_BANKS < 2 * MT:
+                    transposes(n + XT_BANKS)
+
+            def spread(col, name):
+                bc = psa.tile([P, P], F32, name=name, tag="bc", bufs=1)
+                nc.tensor.matmul(out=bc[:], lhsT=col.to_broadcast([P, P]), rhs=idsc[:],
+                                 start=True, stop=True)
+                return bc
+
+            def scale_of(bc, r_, s_):
+                nc.vector.tensor_reduce(out=r_[:], in_=bc[:], axis=AX.X, op=ALU.max)
+                nc.vector.reciprocal(out=s_[:], in_=r_[:])
+
+            for n in range(XT_BANKS):
+                transposes(n)
+
+            take_abs(0, 0, K // 2, "V")
+            take_abs(0, K // 2, K, "V")
+            take_abs(0, K, 2 * K, "V")
+            take_max(0)
+            take_abs(1, 0, K, "A")
+            take_abs(1, K, 2 * K, "V")
+            take_abs(2, 0, K, "A")
+            take_abs(2, K, 2 * K, "V")
+            take_max(1)
+            take_abs(3, 0, K, "A")
+            take_abs(3, K, 2 * K, "V")
+            take_max(2)
+            take_abs(4, 0, K, "A")
+            take_abs(4, K, 2 * K, "A")
+            take_max(3)
+            bcx = spread(cols[:, 3:4], "bcx")
+            take_abs(5, 0, 2 * K, "V")
+            scale_of(bcx, xr, xs)
+            for n in range(MT):
+                evict_x(n)
+            take_max(4)
+            for k in (6, 7, 8):
+                take_abs(k, 0, 2 * K, "V")
+                take_max(k - 1)
+            take_abs(9, 0, K, "A")
+            take_abs(9, K, 2 * K, "A")
+            for n in range(MT, 2 * MT):
+                evict_x(n)
+            take_max(8)
+            for k in (10, 11):
+                take_abs(k, 0, 2 * K, "V")
+                take_max(k - 1)
+            take_max(11)
+            bcw = spread(cols[:, 11:12], "bcw")
             quantise_x(0)
-            nc.vector.tensor_reduce(out=wgm[:], in_=bcw[:], axis=AX.X, op=ALU.max)
-            nc.vector.tensor_scalar(out=wr[:], in0=wgm[:], scalar1=EPS, scalar2=1.0 / FP8_MAX,
-                                    op0=ALU.max, op1=ALU.mult)
-            nc.vector.reciprocal(out=ws[:], in_=wr[:])
+            scale_of(bcw, wr, ws)
 
         w4 = w_raw[:].rearrange("p c (e n) -> p (c e) n", e=2)
+        wgs = {}
 
-        def regroup_w(j, g):
+        def regroup_w(j, g, eng):
             wg = t4k.tile([P, 4 * NW], BF16, name="wg", tag="t4k", align_bytes=64)
             src = w4[:, 4 * g:4 * g + 4, j * NW:(j + 1) * NW].rearrange("p t (c i) -> p c t i", i=4)
             dst = wg[:].rearrange("p (c i t) -> p c t i", i=4, t=4)
-            if W_REG[j][g] == "V":
+            if eng == "V":
                 nc.vector.tensor_scalar(out=dst, in0=src, scalar1=ws[:, 0:1], scalar2=None,
                                         op0=ALU.mult)
             else:
                 nc.scalar.activation(out=dst, in_=src, func=ACTF.Copy, scale=ws[:, 0:1])
-            return wg
+            wgs[(j, g)] = wg
 
-        def quantise_w(j, g, wg):
+        def quantise_w(j, g):
             b = (j * G + g) * NW
             nc.vector.quantize_mx(out=wc[:, b:b + NW].bitcast(FP8X4), scales=wp[:, b:b + NW],
-                                  in_=wg[:])
+                                  in_=wgs[(j, g)][:])
 
         def mx_pass(acc, i, j, g):
             a = (g * MT + i) * P
@@ -154,9 +200,9 @@ def tile_modelnew_kernel(tc, x, weight, out):
                                 rhs=wc[:, b:b + NW].bitcast(FP8X4), rhs_scale=wp[:, b:b + NW],
                                 start=(g == 0), stop=(g == G - 1))
 
-        def finish(acc, i, j):
+        def finish(acc, i, j, eng):
             o = ostp.tile([P, NW], F32, name="o", tag="o")
-            if i % 4 == 3:
+            if eng == "V":
                 nc.vector.tensor_scalar(out=o[:], in0=acc[:], scalar1=inv[:, 0:1], scalar2=None,
                                         op0=ALU.mult)
             else:
@@ -164,29 +210,40 @@ def tile_modelnew_kernel(tc, x, weight, out):
             nc.sync.dma_start(out=ov[:, i, j * NW:(j + 1) * NW], in_=o[:])
 
         with tc.psum_pool(name="psb", bufs=8) as psb:
-            accs = []
+            regroup_w(0, 0, "V")
+            quantise_w(0, 0)
+            regroup_w(0, 1, "A")
+            quantise_x(1)
+            quantise_w(0, 1)
+            regroup_w(0, 2, "V")
+            quantise_x(2)
+            quantise_w(0, 2)
+            regroup_w(0, 3, "A")
+            quantise_x(3)
+            quantise_w(0, 3)
+            accs = {}
             for i in range(MT):
                 acc0 = psb.tile([P, NW], F32, name="acc", tag="acc")
-                accs.append(acc0)
+                accs[i] = acc0
             for g in range(G):
-                wg = regroup_w(0, g)
-                if g > 0:
-                    quantise_x(g)
-                quantise_w(0, g, wg)
                 for i in range(MT):
                     mx_pass(accs[i], i, 0, g)
             nc.vector.tensor_tensor(out=inv[:], in0=xr[:], in1=wr[:], op=ALU.mult)
             for j in range(1, NJ):
-                wgs = []
-                for g in range(G):
-                    wgs.append(regroup_w(j, g))
-                for g in range(G):
-                    quantise_w(j, g, wgs[g])
-                if j == 1:
-                    for i in range(MT):
-                        finish(accs[i], i, 0)
+                regroup_w(j, 3, "A")
+                regroup_w(j, 0, "V")
+                regroup_w(j, 1, "V")
+                quantise_w(j, 0)
+                regroup_w(j, 2, "V")
+                quantise_w(j, 1)
+                quantise_w(j, 2)
+                quantise_w(j, 3)
+                for i in range(MT):
+                    finish(accs[i], i, j - 1, "A")
                 for i in range(MT):
                     acc = psb.tile([P, NW], F32, name="acc", tag="acc")
+                    accs[i] = acc
                     for g in range(G):
                         mx_pass(acc, i, j, g)
-                    finish(acc, i, j)
+            for i in range(MT):
+                finish(accs[i], i, NJ - 1, "V" if i % 2 else "A")

@@ -49,6 +49,8 @@ def tile_modelnew_kernel(tc, x, weight, out):
         wp = keep.tile([P, NJ * G * NW], U8, align_bytes=64)
         ident = keep.tile([P, P], F32)
         idsc = keep.tile([P, P], F32)
+        xcols = keep.tile([P, MT + 1], F32)
+        xm = keep.tile([P, 1], F32)
         cols = keep.tile([P, 12], F32)
         xr = keep.tile([P, 1], F32)
         wr = keep.tile([P, 1], F32)
@@ -57,6 +59,7 @@ def tile_modelnew_kernel(tc, x, weight, out):
         inv = keep.tile([P, 1], F32)
 
         make_identity(nc, ident[:])
+        nc.vector.memset(xcols[:, MT:MT + 1], EPS)
         nc.vector.tensor_scalar(out=idsc[:], in0=ident[:], scalar1=1.0 / FP8_MAX, scalar2=None,
                                 op0=ALU.mult)
 
@@ -93,14 +96,19 @@ def tile_modelnew_kernel(tc, x, weight, out):
 
         def take_max(k):
             s = groups[k]
-            start = EPS if k in (0, 4) else cols[:, k - 1:k]
+            start = EPS if k == 4 else cols[:, k - 1:k]
             nc.vector.tensor_scalar(out=s[:], in0=s[:], scalar1=1.0, scalar2=start,
                                     op0=ALU.mult, op1=ALU.max, accum_out=cols[:, k:k + 1])
 
-        def quantise_x(g):
-            nc.vector.quantize_mx(out=xc[:, g * MT * P:(g + 1) * MT * P].bitcast(FP8X4),
-                                  scales=xp[:, g * MT * P:(g + 1) * MT * P],
-                                  in_=xga[:, g].rearrange("p i c -> p (i c)"))
+        def take_max_x(i):
+            s = groups[i // 2][:, (i % 2) * K:(i % 2 + 1) * K]
+            nc.vector.tensor_scalar(out=s, in0=s, scalar1=1.0, scalar2=None,
+                                    op0=ALU.mult, op1=ALU.max, accum_out=xcols[:, i:i + 1])
+
+        def quantise_x(g, i0, i1):
+            a0, a1 = (g * MT + i0) * P, (g * MT + i1) * P
+            nc.vector.quantize_mx(out=xc[:, a0:a1].bitcast(FP8X4), scales=xp[:, a0:a1],
+                                  in_=xga[:, g, i0:i1, :].rearrange("p i c -> p (i c)"))
 
         with tc.psum_pool(name="psa", bufs=XT_BANKS) as psa:
             banks = {}
@@ -139,20 +147,25 @@ def tile_modelnew_kernel(tc, x, weight, out):
 
             take_abs(0, 0, K // 2, "V")
             take_abs(0, K // 2, K, "V")
+            take_max_x(0)
             take_abs(0, K, 2 * K, "V")
-            take_max(0)
+            take_max_x(1)
             take_abs(1, 0, K, "A")
             take_abs(1, K, 2 * K, "V")
+            take_max_x(3)
             take_abs(2, 0, K, "A")
             take_abs(2, K, 2 * K, "V")
-            take_max(1)
+            take_max_x(2)
+            take_max_x(5)
             take_abs(3, 0, K, "A")
             take_abs(3, K, 2 * K, "V")
-            take_max(2)
+            take_max_x(4)
+            take_max_x(7)
             take_abs(4, 0, K, "A")
             take_abs(4, K, 2 * K, "A")
-            take_max(3)
-            bcx = spread(cols[:, 3:4], "bcx")
+            take_max_x(6)
+            nc.vector.tensor_reduce(out=xm[:], in_=xcols[:], axis=AX.X, op=ALU.max)
+            bcx = spread(xm[:, 0:1], "bcx")
             take_abs(5, 0, 2 * K, "V")
             scale_of(bcx, xr, xs)
             for n in range(MT):
@@ -171,7 +184,7 @@ def tile_modelnew_kernel(tc, x, weight, out):
                 take_max(k - 1)
             take_max(11)
             bcw = spread(cols[:, 11:12], "bcw")
-            quantise_x(0)
+            quantise_x(0, 0, MT // 2)
             scale_of(bcw, wr, ws)
 
         w4 = w_raw[:].rearrange("p c (e n) -> p (c e) n", e=2)
@@ -193,34 +206,33 @@ def tile_modelnew_kernel(tc, x, weight, out):
             nc.vector.quantize_mx(out=wc[:, b:b + NW].bitcast(FP8X4), scales=wp[:, b:b + NW],
                                   in_=wgs[(j, g)][:])
 
-        def mx_pass(acc, i, j, g):
+        def mx_pass(acc, i, j, g, c0=0, c1=NW):
             a = (g * MT + i) * P
             b = (j * G + g) * NW
             nc.tensor.matmul_mx(out=acc[:], lhsT=xc[:, a:a + P].bitcast(FP8X4), lhsT_scale=xp[:, a:a + P],
-                                rhs=wc[:, b:b + NW].bitcast(FP8X4), rhs_scale=wp[:, b:b + NW],
+                                rhs=wc[:, b + c0:b + c1].bitcast(FP8X4), rhs_scale=wp[:, b + c0:b + c1],
                                 start=(g == 0), stop=(g == G - 1))
 
-        def finish(acc, i, j, eng):
+        def finish(acc, i, j, eng, c0=0, c1=NW):
             o = ostp.tile([P, NW], F32, name="o", tag="o")
             if eng == "V":
-                nc.vector.tensor_scalar(out=o[:], in0=acc[:], scalar1=inv[:, 0:1], scalar2=None,
-                                        op0=ALU.mult)
+                nc.vector.tensor_scalar(out=o[:, c0:c1], in0=acc[:], scalar1=inv[:, 0:1],
+                                        scalar2=None, op0=ALU.mult)
             else:
-                nc.scalar.activation(out=o[:], in_=acc[:], func=ACTF.Copy, scale=inv[:, 0:1])
-            nc.sync.dma_start(out=ov[:, i, j * NW:(j + 1) * NW], in_=o[:])
+                nc.scalar.activation(out=o[:, c0:c1], in_=acc[:], func=ACTF.Copy,
+                                     scale=inv[:, 0:1])
+            nc.sync.dma_start(out=ov[:, i, j * NW + c0:j * NW + c1], in_=o[:, c0:c1])
 
         with tc.psum_pool(name="psb", bufs=8) as psb:
             regroup_w(0, 0, "V")
             quantise_w(0, 0)
             regroup_w(0, 1, "A")
-            quantise_x(1)
-            quantise_w(0, 1)
-            regroup_w(0, 2, "V")
-            quantise_x(2)
-            quantise_w(0, 2)
+            regroup_w(0, 2, "A")
             regroup_w(0, 3, "A")
-            quantise_x(3)
-            quantise_w(0, 3)
+            quantise_x(0, MT // 2, MT)
+            for g in range(1, G):
+                quantise_x(g, 0, MT)
+                quantise_w(0, g)
             accs = {}
             for i in range(MT):
                 acc0 = psb.tile([P, NW], F32, name="acc", tag="acc")
@@ -230,20 +242,29 @@ def tile_modelnew_kernel(tc, x, weight, out):
                     mx_pass(accs[i], i, 0, g)
             nc.vector.tensor_tensor(out=inv[:], in0=xr[:], in1=wr[:], op=ALU.mult)
             for j in range(1, NJ):
-                regroup_w(j, 3, "A")
-                regroup_w(j, 0, "V")
-                regroup_w(j, 1, "V")
-                quantise_w(j, 0)
-                regroup_w(j, 2, "V")
-                quantise_w(j, 1)
-                quantise_w(j, 2)
-                quantise_w(j, 3)
+                first_a = 2 if j == 1 else 3
+                for g in range(first_a, G):
+                    regroup_w(j, g, "A")
+                for g in range(first_a):
+                    regroup_w(j, g, "V")
+                    if g > 0:
+                        quantise_w(j, g - 1)
+                for g in range(first_a - 1, G):
+                    quantise_w(j, g)
                 for i in range(MT):
                     finish(accs[i], i, j - 1, "A")
                 for i in range(MT):
+                    if j == NJ - 1 and i == MT - 1:
+                        break
                     acc = psb.tile([P, NW], F32, name="acc", tag="acc")
                     accs[i] = acc
                     for g in range(G):
                         mx_pass(acc, i, j, g)
-            for i in range(MT):
+            for i in range(MT - 1):
                 finish(accs[i], i, NJ - 1, "V" if i % 2 else "A")
+            for half in range(2):
+                c0 = half * (NW // 2)
+                acc_h = psb.tile([P, NW // 2], F32, name="acch", tag="acc")
+                for g in range(G):
+                    mx_pass(acc_h, MT - 1, NJ - 1, g, c0, c0 + NW // 2)
+                finish(acc_h, MT - 1, NJ - 1, "V" if half == 0 else "A", c0, c0 + NW // 2)

@@ -23,7 +23,7 @@ FP8_MAX = 448.0
 EPS = 1e-12
 ABS_MASK = 0x7FFF7FFF
 XT_BANKS = 7
-DUMMIES = 0
+DUMMIES = 4
 
 FLOPS = 2 * M * K * N
 
@@ -37,8 +37,8 @@ def tile_modelnew_kernel(tc, x, weight, out):
     with ExitStack() as ctx:
         keep = ctx.enter_context(tc.tile_pool(name="keep", bufs=1))
         t4k = ctx.enter_context(tc.tile_pool(name="t4k", bufs=8))
-        scr = ctx.enter_context(tc.tile_pool(name="scr", bufs=3))
-        ostp = ctx.enter_context(tc.tile_pool(name="ostp", bufs=6))
+        scr = ctx.enter_context(tc.tile_pool(name="scr", bufs=2))
+        ostp = ctx.enter_context(tc.tile_pool(name="ostp", bufs=5))
         ctx.enter_context(tc.manual_schedule())
 
         w_raw = keep.tile([P, 2 * G, 2 * N], BF16)
@@ -77,31 +77,41 @@ def tile_modelnew_kernel(tc, x, weight, out):
 
         groups = {}
 
-        def unit_src(k, lo, hi):
-            if k >= 4:
-                return w_raw[:, k - 4, lo:hi]
-            return x_raw[2 * k + lo // K][:, lo % K:(hi - 1) % K + 1]
+        def unit_src(u0, u1):
+            if u0 < MT:
+                return x_raw[u0][:]
+            c = (u0 - MT) // 2
+            lo = ((u0 - MT) % 2) * K
+            return w_raw[:, c, lo:lo + (u1 - u0) * K]
 
-        def take_abs(k, lo, hi, eng):
-            if k not in groups:
-                s_new = scr.tile([P, 2 * K], BF16, name="s", tag="s")
-                groups[k] = s_new
-            dst = groups[k][:, lo:hi]
-            src = unit_src(k, lo, hi)
+        def scratch(u0, u1):
+            t = u0 // 4
+            if t not in groups:
+                s_new = scr.tile([P, 4 * K], BF16, name="s", tag="s")
+                groups[t] = s_new
+            return groups[t][:, (u0 % 4) * K:(u0 % 4 + u1 - u0) * K]
+
+        def take_abs(u0, u1, eng, c0=0, c1=0):
+            dst = scratch(u0, u1)
+            src = unit_src(u0, u1)
+            if c1 > 0:
+                dst = dst[:, c0:c1]
+                src = src[:, c0:c1]
             if eng == "V":
                 nc.vector.tensor_scalar(out=dst.bitcast(I32), in0=src.bitcast(I32),
                                         scalar1=ABS_MASK, scalar2=None, op0=ALU.bitwise_and)
             else:
                 nc.scalar.activation(out=dst, in_=src, func=ACTF.Abs)
 
-        def take_max(k):
-            s = groups[k]
-            start = EPS if k == 4 else cols[:, k - 1:k]
-            nc.vector.tensor_scalar(out=s[:], in0=s[:], scalar1=1.0, scalar2=start,
-                                    op0=ALU.mult, op1=ALU.max, accum_out=cols[:, k:k + 1])
+        def take_max(u0, u1):
+            s = scratch(u0, u1)
+            n = (u0 - MT) // 4
+            start = EPS if n == 0 else cols[:, n - 1:n]
+            nc.vector.tensor_scalar(out=s, in0=s, scalar1=1.0, scalar2=start,
+                                    op0=ALU.mult, op1=ALU.max, accum_out=cols[:, n:n + 1])
 
         def take_max_x(i):
-            s = groups[i // 2][:, (i % 2) * K:(i % 2 + 1) * K]
+            s = scratch(i, i + 1)
             nc.vector.tensor_scalar(out=s, in0=s, scalar1=1.0, scalar2=None,
                                     op0=ALU.mult, op1=ALU.max, accum_out=xcols[:, i:i + 1])
 
@@ -145,45 +155,50 @@ def tile_modelnew_kernel(tc, x, weight, out):
             for n in range(XT_BANKS):
                 transposes(n)
 
-            take_abs(0, 0, K // 2, "V")
-            take_abs(0, K // 2, K, "V")
+            take_abs(0, 1, "V", 0, K // 2)
+            take_abs(0, 1, "V", K // 2, K)
             take_max_x(0)
-            take_abs(0, K, 2 * K, "V")
+            take_abs(1, 2, "V")
             take_max_x(1)
-            take_abs(1, 0, K, "A")
-            take_abs(1, K, 2 * K, "V")
+            take_abs(2, 3, "A")
+            take_abs(3, 4, "V")
             take_max_x(3)
-            take_abs(2, 0, K, "A")
-            take_abs(2, K, 2 * K, "V")
+            take_abs(4, 5, "A")
+            take_abs(5, 6, "V")
             take_max_x(2)
             take_max_x(5)
-            take_abs(3, 0, K, "A")
-            take_abs(3, K, 2 * K, "V")
+            take_abs(6, 7, "A")
+            take_abs(7, 8, "V")
             take_max_x(4)
             take_max_x(7)
-            take_abs(4, 0, K, "A")
-            take_abs(4, K, 2 * K, "A")
+            take_abs(8, 9, "A")
+            take_abs(9, 10, "A")
             take_max_x(6)
             nc.vector.tensor_reduce(out=xm[:], in_=xcols[:], axis=AX.X, op=ALU.max)
             bcx = spread(xm[:, 0:1], "bcx")
-            take_abs(5, 0, 2 * K, "V")
+            take_abs(10, 12, "V")
             scale_of(bcx, xr, xs)
             for n in range(MT):
                 evict_x(n)
-            take_max(4)
-            for k in (6, 7, 8):
-                take_abs(k, 0, 2 * K, "V")
-                take_max(k - 1)
-            take_abs(9, 0, K, "A")
-            take_abs(9, K, 2 * K, "A")
+            take_abs(12, 14, "V")
+            take_max(8, 12)
+            take_abs(14, 16, "V")
+            take_abs(16, 18, "V")
+            take_abs(18, 19, "A")
+            take_abs(19, 20, "A")
             for n in range(MT, 2 * MT):
                 evict_x(n)
-            take_max(8)
-            for k in (10, 11):
-                take_abs(k, 0, 2 * K, "V")
-                take_max(k - 1)
-            take_max(11)
-            bcw = spread(cols[:, 11:12], "bcw")
+            take_max(12, 16)
+            take_abs(20, 22, "V")
+            take_abs(22, 24, "V")
+            take_max(16, 20)
+            take_max(20, 24)
+            bcw = spread(cols[:, 3:4], "bcw")
+            if DUMMIES > 0:
+                warm = psa.tile([P, NW], F32, name="warm", tag="xt")
+                for d in range(DUMMIES):
+                    nc.tensor.matmul(out=warm[:], lhsT=w_raw[:, 0, 0:P], rhs=w_raw[:, 0, 0:NW],
+                                     start=True, stop=True)
             quantise_x(0, 0, MT // 2)
             scale_of(bcw, wr, ws)
 

@@ -15,271 +15,280 @@ AX = mybir.AxisListType
 
 P = 128
 M, K, N = 1024, 2048, 2048
-MT = M // P
-G = K // 512
-NW = 512
-NJ = N // NW
+ROW_TILES = M // P
+PACK = 4
+PASSES = K // (P * PACK)
+CHUNK = 512
+CHUNKS = N // CHUNK
+W_LOADS = 2 * PASSES
+UNIT = 2048
+UNITS_PER_SCRATCH = 4
+W_MAXIMA = 2 * W_LOADS // UNITS_PER_SCRATCH
+PAIRS = P
+RUN = 4
 FP8_MAX = 448.0
 EPS = 1e-12
-ABS_MASK = 0x7FFF7FFF
-XT_BANKS = 7
-DUMMIES = 4
+SIGN_BITS_OFF = 0x7FFF7FFF
+TRANSPOSE_BANKS = 7
+WARM_UP_MATMULS = 4
 
 FLOPS = 2 * M * K * N
 
 
 def tile_modelnew_kernel(tc, x, weight, out):
     nc = tc.nc
-    xv = x.flatten_outer_dims().rearrange("(p i) k -> p i k", i=MT)
-    ov = out.flatten_outer_dims().rearrange("(p i) n -> p i n", i=MT)
-    wv = weight.rearrange("(c p e) n -> p c (e n)", p=P, e=2)
+    x_rows = x.flatten_outer_dims().rearrange("(p i) k -> p i k", i=ROW_TILES)
+    out_rows = out.flatten_outer_dims().rearrange("(p i) n -> p i n", i=ROW_TILES)
+    w_rows = weight.rearrange("(c p e) n -> p c (e n)", p=P, e=2)
 
     with ExitStack() as ctx:
         keep = ctx.enter_context(tc.tile_pool(name="keep", bufs=1))
-        t4k = ctx.enter_context(tc.tile_pool(name="t4k", bufs=8))
-        scr = ctx.enter_context(tc.tile_pool(name="scr", bufs=2))
-        ostp = ctx.enter_context(tc.tile_pool(name="ostp", bufs=5))
+        slots = ctx.enter_context(tc.tile_pool(name="slots", bufs=ROW_TILES))
+        scratch_pool = ctx.enter_context(tc.tile_pool(name="scratch", bufs=2))
+        out_pool = ctx.enter_context(tc.tile_pool(name="outs", bufs=5))
         ctx.enter_context(tc.manual_schedule())
 
-        w_raw = keep.tile([P, 2 * G, 2 * N], BF16)
-        xga = keep.tile([P, G, MT, 4 * P], BF16, align_bytes=64)
-        xc = keep.tile([P, G * MT * P], U32, align_bytes=64)
-        xp = keep.tile([P, G * MT * P], U8, align_bytes=64)
-        wc = keep.tile([P, NJ * G * NW], U32, align_bytes=64)
-        wp = keep.tile([P, NJ * G * NW], U8, align_bytes=64)
-        ident = keep.tile([P, P], F32)
-        idsc = keep.tile([P, P], F32)
-        xcols = keep.tile([P, MT + 1], F32)
-        xm = keep.tile([P, 1], F32)
-        cols = keep.tile([P, 12], F32)
-        xr = keep.tile([P, 1], F32)
-        wr = keep.tile([P, 1], F32)
+        w_sb = keep.tile([P, W_LOADS, 2 * N], BF16)
+        x_sim = keep.tile([P, PASSES, ROW_TILES, PACK * P], BF16, align_bytes=64)
+        x_codes = keep.tile([P, PASSES * ROW_TILES * P], U32, align_bytes=64)
+        x_scale_bytes = keep.tile([P, PASSES * ROW_TILES * P], U8, align_bytes=64)
+        w_codes = keep.tile([P, CHUNKS * PASSES * CHUNK], U32, align_bytes=64)
+        w_scale_bytes = keep.tile([P, CHUNKS * PASSES * CHUNK], U8, align_bytes=64)
+        identity = keep.tile([P, P], F32)
+        identity_over_448 = keep.tile([P, P], F32)
+        x_unit_max = keep.tile([P, ROW_TILES + 1], F32)
+        x_part_max = keep.tile([P, 1], F32)
+        w_part_max = keep.tile([P, W_MAXIMA], F32)
+        x_max_over_448 = keep.tile([P, 1], F32)
+        w_max_over_448 = keep.tile([P, 1], F32)
         xs = keep.tile([P, 1], F32)
         ws = keep.tile([P, 1], F32)
-        inv = keep.tile([P, 1], F32)
+        out_factor = keep.tile([P, 1], F32)
 
-        make_identity(nc, ident[:])
-        nc.vector.memset(xcols[:, MT:MT + 1], EPS)
-        nc.vector.tensor_scalar(out=idsc[:], in0=ident[:], scalar1=1.0 / FP8_MAX, scalar2=None,
-                                op0=ALU.mult)
+        make_identity(nc, identity[:])
+        nc.vector.memset(x_unit_max[:, ROW_TILES:ROW_TILES + 1], EPS)
+        nc.vector.tensor_scalar(out=identity_over_448[:], in0=identity[:], scalar1=1.0 / FP8_MAX,
+                                scalar2=None, op0=ALU.mult)
 
-        x_raw = []
-        for i in range(MT):
-            xt_i = t4k.tile([P, K], BF16, name="xraw%d" % i, tag="t4k", align_bytes=64)
+        x_sb = []
+        for i in range(ROW_TILES):
+            x_tile = slots.tile([P, K], BF16, name="x_tile%d" % i, tag="slot", align_bytes=64)
             if i == 0:
-                nc.sync.dma_start(out=xt_i[:, 0:K // 2], in_=xv[:, i, 0:K // 2])
-                nc.sync.dma_start(out=xt_i[:, K // 2:K], in_=xv[:, i, K // 2:K])
+                nc.sync.dma_start(out=x_tile[:, 0:K // 2], in_=x_rows[:, i, 0:K // 2])
+                nc.sync.dma_start(out=x_tile[:, K // 2:K], in_=x_rows[:, i, K // 2:K])
             else:
-                nc.sync.dma_start(out=xt_i[:], in_=xv[:, i, :])
-            x_raw.append(xt_i)
-        for c in range(2 * G):
-            nc.sync.dma_start(out=w_raw[:, c, :], in_=wv[:, c, :])
+                nc.sync.dma_start(out=x_tile[:], in_=x_rows[:, i, :])
+            x_sb.append(x_tile)
+        for c in range(W_LOADS):
+            nc.sync.dma_start(out=w_sb[:, c, :], in_=w_rows[:, c, :])
 
-        groups = {}
+        scratch_tiles = {}
 
-        def unit_src(u0, u1):
-            if u0 < MT:
-                return x_raw[u0][:]
-            c = (u0 - MT) // 2
-            lo = ((u0 - MT) % 2) * K
-            return w_raw[:, c, lo:lo + (u1 - u0) * K]
+        def raw_units(u0, u1):
+            if u0 < ROW_TILES:
+                return x_sb[u0][:]
+            c = (u0 - ROW_TILES) // 2
+            lo = ((u0 - ROW_TILES) % 2) * UNIT
+            return w_sb[:, c, lo:lo + (u1 - u0) * UNIT]
 
-        def scratch(u0, u1):
-            t = u0 // 4
-            if t not in groups:
-                s_new = scr.tile([P, 4 * K], BF16, name="s", tag="s")
-                groups[t] = s_new
-            return groups[t][:, (u0 % 4) * K:(u0 % 4 + u1 - u0) * K]
+        def magnitudes(u0, u1):
+            t = u0 // UNITS_PER_SCRATCH
+            if t not in scratch_tiles:
+                new_scratch = scratch_pool.tile([P, UNITS_PER_SCRATCH * UNIT], BF16, name="magnitudes",
+                                                tag="magnitudes")
+                scratch_tiles[t] = new_scratch
+            first = u0 % UNITS_PER_SCRATCH
+            return scratch_tiles[t][:, first * UNIT:(first + u1 - u0) * UNIT]
 
-        def take_abs(u0, u1, eng, c0=0, c1=0):
-            dst = scratch(u0, u1)
-            src = unit_src(u0, u1)
-            if c1 > 0:
-                dst = dst[:, c0:c1]
-                src = src[:, c0:c1]
-            if eng == "V":
+        def clear_signs(u0, u1, engine, columns=None):
+            dst = magnitudes(u0, u1)
+            src = raw_units(u0, u1)
+            if columns is not None:
+                dst = dst[:, columns]
+                src = src[:, columns]
+            if engine == "vector":
                 nc.vector.tensor_scalar(out=dst.bitcast(I32), in0=src.bitcast(I32),
-                                        scalar1=ABS_MASK, scalar2=None, op0=ALU.bitwise_and)
+                                        scalar1=SIGN_BITS_OFF, scalar2=None, op0=ALU.bitwise_and)
             else:
                 nc.scalar.activation(out=dst, in_=src, func=ACTF.Abs)
 
-        def take_max(u0, u1):
-            s = scratch(u0, u1)
-            n = (u0 - MT) // 4
-            start = EPS if n == 0 else cols[:, n - 1:n]
-            nc.vector.tensor_scalar(out=s, in0=s, scalar1=1.0, scalar2=start,
-                                    op0=ALU.mult, op1=ALU.max, accum_out=cols[:, n:n + 1])
+        def max_of_w_units(u0, u1):
+            mags = magnitudes(u0, u1)
+            n = (u0 - ROW_TILES) // UNITS_PER_SCRATCH
+            first_value = EPS if n == 0 else w_part_max[:, n - 1:n]
+            nc.vector.tensor_scalar(out=mags, in0=mags, scalar1=1.0, scalar2=first_value,
+                                    op0=ALU.mult, op1=ALU.max, accum_out=w_part_max[:, n:n + 1])
 
-        def take_max_x(i):
-            s = scratch(i, i + 1)
-            nc.vector.tensor_scalar(out=s, in0=s, scalar1=1.0, scalar2=None,
-                                    op0=ALU.mult, op1=ALU.max, accum_out=xcols[:, i:i + 1])
+        def max_of_x_unit(i):
+            mags = magnitudes(i, i + 1)
+            nc.vector.tensor_scalar(out=mags, in0=mags, scalar1=1.0, scalar2=None,
+                                    op0=ALU.mult, op1=ALU.max, accum_out=x_unit_max[:, i:i + 1])
 
         def quantise_x(g, i0, i1):
-            a0, a1 = (g * MT + i0) * P, (g * MT + i1) * P
-            nc.vector.quantize_mx(out=xc[:, a0:a1].bitcast(FP8X4), scales=xp[:, a0:a1],
-                                  in_=xga[:, g, i0:i1, :].rearrange("p i c -> p (i c)"))
+            a0, a1 = (g * ROW_TILES + i0) * P, (g * ROW_TILES + i1) * P
+            nc.vector.quantize_mx(out=x_codes[:, a0:a1].bitcast(FP8X4), scales=x_scale_bytes[:, a0:a1],
+                                  in_=x_sim[:, g, i0:i1, :].rearrange("p i c -> p (i c)"))
 
-        with tc.psum_pool(name="psa", bufs=XT_BANKS) as psa:
-            banks = {}
+        with tc.psum_pool(name="psum1", bufs=TRANSPOSE_BANKS) as psum1:
+            transposed = {}
 
-            def transposes(n):
-                h, i = n // MT, n % MT
-                xw = x_raw[i][:].bitcast(F32)
-                xt = psa.tile([P, 2, 2, P], F32, name="xt", tag="xt")
+            def transpose_x(n):
+                h, i = n // ROW_TILES, n % ROW_TILES
+                pairs = x_sb[i][:].bitcast(F32)
+                bank = psum1.tile([P, 2, 2, P], F32, name="bank", tag="bank")
                 for gg in range(2):
                     for u in range(2):
-                        w0 = 256 * (2 * h + gg) + 128 * u
-                        nc.tensor.transpose(xt[:, u, gg, :], xw[:, w0:w0 + P], ident[:])
-                banks[n] = xt
+                        first = PAIRS * (2 * (2 * h + gg) + u)
+                        nc.tensor.transpose(bank[:, u, gg, :], pairs[:, first:first + PAIRS], identity[:])
+                transposed[n] = bank
 
-            def evict_x(n):
-                h, i = n // MT, n % MT
+            def scale_x(n):
+                h, i = n // ROW_TILES, n % ROW_TILES
                 nc.scalar.activation(
-                    out=xga[:, 2 * h:2 * h + 2, i, :].rearrange("p g (r u e) -> p g r u e", u=2, e=2),
-                    in_=banks[n][:].bitcast(BF16).rearrange("p u g (r e) -> p g r u e", e=2),
+                    out=x_sim[:, 2 * h:2 * h + 2, i, :].rearrange("p g (r u e) -> p g r u e", u=2, e=2),
+                    in_=transposed[n][:].bitcast(BF16).rearrange("p u g (r e) -> p g r u e", e=2),
                     func=ACTF.Copy, scale=xs[:, 0:1])
-                if n + XT_BANKS < 2 * MT:
-                    transposes(n + XT_BANKS)
+                if n + TRANSPOSE_BANKS < 2 * ROW_TILES:
+                    transpose_x(n + TRANSPOSE_BANKS)
 
-            def spread(col, name):
-                bc = psa.tile([P, P], F32, name=name, tag="bc", bufs=1)
-                nc.tensor.matmul(out=bc[:], lhsT=col.to_broadcast([P, P]), rhs=idsc[:],
+            def spread(column, name):
+                everywhere = psum1.tile([P, P], F32, name=name, tag="spread", bufs=1)
+                nc.tensor.matmul(out=everywhere[:], lhsT=column.to_broadcast([P, P]),
+                                 rhs=identity_over_448[:], start=True, stop=True)
+                return everywhere
+
+            def scale_from(everywhere, max_over_448, scale):
+                nc.vector.tensor_reduce(out=max_over_448[:], in_=everywhere[:], axis=AX.X, op=ALU.max)
+                nc.vector.reciprocal(out=scale[:], in_=max_over_448[:])
+
+            for n in range(TRANSPOSE_BANKS):
+                transpose_x(n)
+
+            clear_signs(0, 1, "vector", slice(0, K // 2))
+            clear_signs(0, 1, "vector", slice(K // 2, K))
+            max_of_x_unit(0)
+            clear_signs(1, 2, "vector")
+            max_of_x_unit(1)
+            clear_signs(2, 3, "scalar")
+            clear_signs(3, 4, "vector")
+            max_of_x_unit(3)
+            clear_signs(4, 5, "scalar")
+            clear_signs(5, 6, "vector")
+            max_of_x_unit(2)
+            max_of_x_unit(5)
+            clear_signs(6, 7, "scalar")
+            clear_signs(7, 8, "vector")
+            max_of_x_unit(4)
+            max_of_x_unit(7)
+            clear_signs(8, 10, "scalar")
+            max_of_x_unit(6)
+            nc.vector.tensor_reduce(out=x_part_max[:], in_=x_unit_max[:], axis=AX.X, op=ALU.max)
+            x_everywhere = spread(x_part_max[:, 0:1], "x_everywhere")
+            clear_signs(10, 12, "vector")
+            scale_from(x_everywhere, x_max_over_448, xs)
+            for n in range(ROW_TILES):
+                scale_x(n)
+            clear_signs(12, 14, "vector")
+            max_of_w_units(8, 12)
+            clear_signs(14, 16, "vector")
+            clear_signs(16, 18, "vector")
+            clear_signs(18, 20, "scalar")
+            for n in range(ROW_TILES, 2 * ROW_TILES):
+                scale_x(n)
+            max_of_w_units(12, 16)
+            clear_signs(20, 22, "vector")
+            clear_signs(22, 24, "vector")
+            max_of_w_units(16, 20)
+            max_of_w_units(20, 24)
+            w_everywhere = spread(w_part_max[:, W_MAXIMA - 1:W_MAXIMA], "w_everywhere")
+            warm_up = psum1.tile([P, CHUNK], F32, name="warm_up", tag="bank")
+            for d in range(WARM_UP_MATMULS):
+                nc.tensor.matmul(out=warm_up[:], lhsT=w_sb[:, 0, 0:P], rhs=w_sb[:, 0, 0:CHUNK],
                                  start=True, stop=True)
-                return bc
+            quantise_x(0, 0, ROW_TILES // 2)
+            scale_from(w_everywhere, w_max_over_448, ws)
 
-            def scale_of(bc, r_, s_):
-                nc.vector.tensor_reduce(out=r_[:], in_=bc[:], axis=AX.X, op=ALU.max)
-                nc.vector.reciprocal(out=s_[:], in_=r_[:])
+        w_by_row = w_sb[:].rearrange("p c (e n) -> p (c e) n", e=2)
+        panels = {}
 
-            for n in range(XT_BANKS):
-                transposes(n)
-
-            take_abs(0, 1, "V", 0, K // 2)
-            take_abs(0, 1, "V", K // 2, K)
-            take_max_x(0)
-            take_abs(1, 2, "V")
-            take_max_x(1)
-            take_abs(2, 3, "A")
-            take_abs(3, 4, "V")
-            take_max_x(3)
-            take_abs(4, 5, "A")
-            take_abs(5, 6, "V")
-            take_max_x(2)
-            take_max_x(5)
-            take_abs(6, 7, "A")
-            take_abs(7, 8, "V")
-            take_max_x(4)
-            take_max_x(7)
-            take_abs(8, 9, "A")
-            take_abs(9, 10, "A")
-            take_max_x(6)
-            nc.vector.tensor_reduce(out=xm[:], in_=xcols[:], axis=AX.X, op=ALU.max)
-            bcx = spread(xm[:, 0:1], "bcx")
-            take_abs(10, 12, "V")
-            scale_of(bcx, xr, xs)
-            for n in range(MT):
-                evict_x(n)
-            take_abs(12, 14, "V")
-            take_max(8, 12)
-            take_abs(14, 16, "V")
-            take_abs(16, 18, "V")
-            take_abs(18, 19, "A")
-            take_abs(19, 20, "A")
-            for n in range(MT, 2 * MT):
-                evict_x(n)
-            take_max(12, 16)
-            take_abs(20, 22, "V")
-            take_abs(22, 24, "V")
-            take_max(16, 20)
-            take_max(20, 24)
-            bcw = spread(cols[:, 3:4], "bcw")
-            if DUMMIES > 0:
-                warm = psa.tile([P, NW], F32, name="warm", tag="xt")
-                for d in range(DUMMIES):
-                    nc.tensor.matmul(out=warm[:], lhsT=w_raw[:, 0, 0:P], rhs=w_raw[:, 0, 0:NW],
-                                     start=True, stop=True)
-            quantise_x(0, 0, MT // 2)
-            scale_of(bcw, wr, ws)
-
-        w4 = w_raw[:].rearrange("p c (e n) -> p (c e) n", e=2)
-        wgs = {}
-
-        def regroup_w(j, g, eng):
-            wg = t4k.tile([P, 4 * NW], BF16, name="wg", tag="t4k", align_bytes=64)
-            src = w4[:, 4 * g:4 * g + 4, j * NW:(j + 1) * NW].rearrange("p t (c i) -> p c t i", i=4)
-            dst = wg[:].rearrange("p (c i t) -> p c t i", i=4, t=4)
-            if eng == "V":
+        def scale_w(j, g, engine):
+            panel = slots.tile([P, PACK * CHUNK], BF16, name="panel", tag="slot", align_bytes=64)
+            src = w_by_row[:, PACK * g:PACK * g + PACK, j * CHUNK:(j + 1) * CHUNK].rearrange(
+                "p t (c i) -> p c t i", i=RUN)
+            dst = panel[:].rearrange("p (c i t) -> p c t i", i=RUN, t=PACK)
+            if engine == "vector":
                 nc.vector.tensor_scalar(out=dst, in0=src, scalar1=ws[:, 0:1], scalar2=None,
                                         op0=ALU.mult)
             else:
                 nc.scalar.activation(out=dst, in_=src, func=ACTF.Copy, scale=ws[:, 0:1])
-            wgs[(j, g)] = wg
+            panels[(j, g)] = panel
 
         def quantise_w(j, g):
-            b = (j * G + g) * NW
-            nc.vector.quantize_mx(out=wc[:, b:b + NW].bitcast(FP8X4), scales=wp[:, b:b + NW],
-                                  in_=wgs[(j, g)][:])
+            b = (j * PASSES + g) * CHUNK
+            nc.vector.quantize_mx(out=w_codes[:, b:b + CHUNK].bitcast(FP8X4), scales=w_scale_bytes[:, b:b + CHUNK],
+                                  in_=panels[(j, g)][:])
 
-        def mx_pass(acc, i, j, g, c0=0, c1=NW):
-            a = (g * MT + i) * P
-            b = (j * G + g) * NW
-            nc.tensor.matmul_mx(out=acc[:], lhsT=xc[:, a:a + P].bitcast(FP8X4), lhsT_scale=xp[:, a:a + P],
-                                rhs=wc[:, b + c0:b + c1].bitcast(FP8X4), rhs_scale=wp[:, b + c0:b + c1],
-                                start=(g == 0), stop=(g == G - 1))
+        def mx_pass(acc, i, j, g, c0=0, c1=CHUNK):
+            a = (g * ROW_TILES + i) * P
+            b = (j * PASSES + g) * CHUNK
+            nc.tensor.matmul_mx(out=acc[:], lhsT=x_codes[:, a:a + P].bitcast(FP8X4),
+                                lhsT_scale=x_scale_bytes[:, a:a + P],
+                                rhs=w_codes[:, b + c0:b + c1].bitcast(FP8X4),
+                                rhs_scale=w_scale_bytes[:, b + c0:b + c1],
+                                start=(g == 0), stop=(g == PASSES - 1))
 
-        def finish(acc, i, j, eng, c0=0, c1=NW):
-            o = ostp.tile([P, NW], F32, name="o", tag="o")
-            if eng == "V":
-                nc.vector.tensor_scalar(out=o[:, c0:c1], in0=acc[:], scalar1=inv[:, 0:1],
+        def finish(acc, i, j, engine, c0=0, c1=CHUNK):
+            result = out_pool.tile([P, CHUNK], F32, name="result", tag="result")
+            if engine == "vector":
+                nc.vector.tensor_scalar(out=result[:, c0:c1], in0=acc[:], scalar1=out_factor[:, 0:1],
                                         scalar2=None, op0=ALU.mult)
             else:
-                nc.scalar.activation(out=o[:, c0:c1], in_=acc[:], func=ACTF.Copy,
-                                     scale=inv[:, 0:1])
-            nc.sync.dma_start(out=ov[:, i, j * NW + c0:j * NW + c1], in_=o[:, c0:c1])
+                nc.scalar.activation(out=result[:, c0:c1], in_=acc[:], func=ACTF.Copy,
+                                     scale=out_factor[:, 0:1])
+            nc.sync.dma_start(out=out_rows[:, i, j * CHUNK + c0:j * CHUNK + c1], in_=result[:, c0:c1])
 
-        with tc.psum_pool(name="psb", bufs=8) as psb:
-            regroup_w(0, 0, "V")
+        with tc.psum_pool(name="psum2", bufs=ROW_TILES) as psum2:
+            scale_w(0, 0, "vector")
             quantise_w(0, 0)
-            regroup_w(0, 1, "A")
-            regroup_w(0, 2, "A")
-            regroup_w(0, 3, "A")
-            quantise_x(0, MT // 2, MT)
-            for g in range(1, G):
-                quantise_x(g, 0, MT)
+            scale_w(0, 1, "scalar")
+            scale_w(0, 2, "scalar")
+            scale_w(0, 3, "scalar")
+            quantise_x(0, ROW_TILES // 2, ROW_TILES)
+            for g in range(1, PASSES):
+                quantise_x(g, 0, ROW_TILES)
                 quantise_w(0, g)
             accs = {}
-            for i in range(MT):
-                acc0 = psb.tile([P, NW], F32, name="acc", tag="acc")
-                accs[i] = acc0
-            for g in range(G):
-                for i in range(MT):
+            for i in range(ROW_TILES):
+                first_acc = psum2.tile([P, CHUNK], F32, name="acc", tag="acc")
+                accs[i] = first_acc
+            for g in range(PASSES):
+                for i in range(ROW_TILES):
                     mx_pass(accs[i], i, 0, g)
-            nc.vector.tensor_tensor(out=inv[:], in0=xr[:], in1=wr[:], op=ALU.mult)
-            for j in range(1, NJ):
-                first_a = 2 if j == 1 else 3
-                for g in range(first_a, G):
-                    regroup_w(j, g, "A")
-                for g in range(first_a):
-                    regroup_w(j, g, "V")
+            nc.vector.tensor_tensor(out=out_factor[:], in0=x_max_over_448[:], in1=w_max_over_448[:],
+                                    op=ALU.mult)
+            for j in range(1, CHUNKS):
+                first_on_scalar = 2 if j == 1 else 3
+                for g in range(first_on_scalar, PASSES):
+                    scale_w(j, g, "scalar")
+                for g in range(first_on_scalar):
+                    scale_w(j, g, "vector")
                     if g > 0:
                         quantise_w(j, g - 1)
-                for g in range(first_a - 1, G):
+                for g in range(first_on_scalar - 1, PASSES):
                     quantise_w(j, g)
-                for i in range(MT):
-                    finish(accs[i], i, j - 1, "A")
-                for i in range(MT):
-                    if j == NJ - 1 and i == MT - 1:
-                        break
-                    acc = psb.tile([P, NW], F32, name="acc", tag="acc")
+                for i in range(ROW_TILES):
+                    finish(accs[i], i, j - 1, "scalar")
+                for i in range(ROW_TILES if j < CHUNKS - 1 else ROW_TILES - 1):
+                    acc = psum2.tile([P, CHUNK], F32, name="acc", tag="acc")
                     accs[i] = acc
-                    for g in range(G):
+                    for g in range(PASSES):
                         mx_pass(acc, i, j, g)
-            for i in range(MT - 1):
-                finish(accs[i], i, NJ - 1, "V" if i % 2 else "A")
+            for i in range(ROW_TILES - 1):
+                finish(accs[i], i, CHUNKS - 1, "vector" if i % 2 else "scalar")
             for half in range(2):
-                c0 = half * (NW // 2)
-                acc_h = psb.tile([P, NW // 2], F32, name="acch", tag="acc")
-                for g in range(G):
-                    mx_pass(acc_h, MT - 1, NJ - 1, g, c0, c0 + NW // 2)
-                finish(acc_h, MT - 1, NJ - 1, "V" if half == 0 else "A", c0, c0 + NW // 2)
+                c0 = half * (CHUNK // 2)
+                half_acc = psum2.tile([P, CHUNK // 2], F32, name="half_acc", tag="acc")
+                for g in range(PASSES):
+                    mx_pass(half_acc, ROW_TILES - 1, CHUNKS - 1, g, c0, c0 + CHUNK // 2)
+                finish(half_acc, ROW_TILES - 1, CHUNKS - 1, "vector" if half == 0 else "scalar",
+                       c0, c0 + CHUNK // 2)

from contextlib import ExitStack

import concourse.mybir as mybir
from concourse.masks import make_identity

BF16 = mybir.dt.bfloat16
F32 = mybir.dt.float32
I32 = mybir.dt.int32
U32 = mybir.dt.uint32
U8 = mybir.dt.uint8
FP8X4 = mybir.dt.float8_e4m3fn_x4
ALU = mybir.AluOpType
ACTF = mybir.ActivationFunctionType
AX = mybir.AxisListType

P = 128
M, K, N = 1024, 2048, 2048
ROW_TILES = M // P
PACK = 4
PASSES = K // (P * PACK)
CHUNK = 512
CHUNKS = N // CHUNK
W_LOADS = 2 * PASSES
UNIT = 2048
UNITS_PER_SCRATCH = 4
W_MAXIMA = 2 * W_LOADS // UNITS_PER_SCRATCH
PAIRS = P
RUN = 4
FP8_MAX = 448.0
EPS = 1e-12
SIGN_BITS_OFF = 0x7FFF7FFF
TRANSPOSE_BANKS = 7
WARM_UP_MATMULS = 4

FLOPS = 2 * M * K * N


def tile_modelnew_kernel(tc, x, weight, out):
    nc = tc.nc
    x_rows = x.flatten_outer_dims().rearrange("(p i) k -> p i k", i=ROW_TILES)
    out_rows = out.flatten_outer_dims().rearrange("(p i) n -> p i n", i=ROW_TILES)
    w_rows = weight.rearrange("(c p e) n -> p c (e n)", p=P, e=2)

    with ExitStack() as ctx:
        keep = ctx.enter_context(tc.tile_pool(name="keep", bufs=1))
        slots = ctx.enter_context(tc.tile_pool(name="slots", bufs=ROW_TILES))
        scratch_pool = ctx.enter_context(tc.tile_pool(name="scratch", bufs=2))
        out_pool = ctx.enter_context(tc.tile_pool(name="outs", bufs=5))
        ctx.enter_context(tc.manual_schedule())

        w_sb = keep.tile([P, W_LOADS, 2 * N], BF16)
        x_sim = keep.tile([P, PASSES, ROW_TILES, PACK * P], BF16, align_bytes=64)
        x_codes = keep.tile([P, PASSES * ROW_TILES * P], U32, align_bytes=64)
        x_scale_bytes = keep.tile([P, PASSES * ROW_TILES * P], U8, align_bytes=64)
        w_codes = keep.tile([P, CHUNKS * PASSES * CHUNK], U32, align_bytes=64)
        w_scale_bytes = keep.tile([P, CHUNKS * PASSES * CHUNK], U8, align_bytes=64)
        identity = keep.tile([P, P], F32)
        identity_over_448 = keep.tile([P, P], F32)
        x_unit_max = keep.tile([P, ROW_TILES + 1], F32)
        x_part_max = keep.tile([P, 1], F32)
        w_part_max = keep.tile([P, W_MAXIMA], F32)
        x_max_over_448 = keep.tile([P, 1], F32)
        w_max_over_448 = keep.tile([P, 1], F32)
        xs = keep.tile([P, 1], F32)
        ws = keep.tile([P, 1], F32)
        out_factor = keep.tile([P, 1], F32)

        make_identity(nc, identity[:])
        nc.vector.memset(x_unit_max[:, ROW_TILES:ROW_TILES + 1], EPS)
        nc.vector.tensor_scalar(out=identity_over_448[:], in0=identity[:], scalar1=1.0 / FP8_MAX,
                                scalar2=None, op0=ALU.mult)

        x_sb = []
        for i in range(ROW_TILES):
            x_tile = slots.tile([P, K], BF16, name="x_tile%d" % i, tag="slot", align_bytes=64)
            if i == 0:
                nc.sync.dma_start(out=x_tile[:, 0:K // 2], in_=x_rows[:, i, 0:K // 2])
                nc.sync.dma_start(out=x_tile[:, K // 2:K], in_=x_rows[:, i, K // 2:K])
            else:
                nc.sync.dma_start(out=x_tile[:], in_=x_rows[:, i, :])
            x_sb.append(x_tile)
        for c in range(W_LOADS):
            nc.sync.dma_start(out=w_sb[:, c, :], in_=w_rows[:, c, :])

        scratch_tiles = {}

        def raw_units(u0, u1):
            if u0 < ROW_TILES:
                return x_sb[u0][:]
            c = (u0 - ROW_TILES) // 2
            lo = ((u0 - ROW_TILES) % 2) * UNIT
            return w_sb[:, c, lo:lo + (u1 - u0) * UNIT]

        def magnitudes(u0, u1):
            t = u0 // UNITS_PER_SCRATCH
            if t not in scratch_tiles:
                new_scratch = scratch_pool.tile([P, UNITS_PER_SCRATCH * UNIT], BF16, name="magnitudes",
                                                tag="magnitudes")
                scratch_tiles[t] = new_scratch
            first = u0 % UNITS_PER_SCRATCH
            return scratch_tiles[t][:, first * UNIT:(first + u1 - u0) * UNIT]

        def clear_signs(u0, u1, engine, columns=None):
            dst = magnitudes(u0, u1)
            src = raw_units(u0, u1)
            if columns is not None:
                dst = dst[:, columns]
                src = src[:, columns]
            if engine == "vector":
                nc.vector.tensor_scalar(out=dst.bitcast(I32), in0=src.bitcast(I32),
                                        scalar1=SIGN_BITS_OFF, scalar2=None, op0=ALU.bitwise_and)
            else:
                nc.scalar.activation(out=dst, in_=src, func=ACTF.Abs)

        def max_of_w_units(u0, u1):
            mags = magnitudes(u0, u1)
            n = (u0 - ROW_TILES) // UNITS_PER_SCRATCH
            first_value = EPS if n == 0 else w_part_max[:, n - 1:n]
            nc.vector.tensor_scalar(out=mags, in0=mags, scalar1=1.0, scalar2=first_value,
                                    op0=ALU.mult, op1=ALU.max, accum_out=w_part_max[:, n:n + 1])

        def max_of_x_unit(i):
            mags = magnitudes(i, i + 1)
            nc.vector.tensor_scalar(out=mags, in0=mags, scalar1=1.0, scalar2=None,
                                    op0=ALU.mult, op1=ALU.max, accum_out=x_unit_max[:, i:i + 1])

        def quantise_x(g, i0, i1):
            a0, a1 = (g * ROW_TILES + i0) * P, (g * ROW_TILES + i1) * P
            nc.vector.quantize_mx(out=x_codes[:, a0:a1].bitcast(FP8X4), scales=x_scale_bytes[:, a0:a1],
                                  in_=x_sim[:, g, i0:i1, :].rearrange("p i c -> p (i c)"))

        with tc.psum_pool(name="psum1", bufs=TRANSPOSE_BANKS) as psum1:
            transposed = {}

            def transpose_x(n):
                h, i = n // ROW_TILES, n % ROW_TILES
                pairs = x_sb[i][:].bitcast(F32)
                bank = psum1.tile([P, 2, 2, P], F32, name="bank", tag="bank")
                for gg in range(2):
                    for u in range(2):
                        first = PAIRS * (2 * (2 * h + gg) + u)
                        nc.tensor.transpose(bank[:, u, gg, :], pairs[:, first:first + PAIRS], identity[:])
                transposed[n] = bank

            def scale_x(n):
                h, i = n // ROW_TILES, n % ROW_TILES
                nc.scalar.activation(
                    out=x_sim[:, 2 * h:2 * h + 2, i, :].rearrange("p g (r u e) -> p g r u e", u=2, e=2),
                    in_=transposed[n][:].bitcast(BF16).rearrange("p u g (r e) -> p g r u e", e=2),
                    func=ACTF.Copy, scale=xs[:, 0:1])
                if n + TRANSPOSE_BANKS < 2 * ROW_TILES:
                    transpose_x(n + TRANSPOSE_BANKS)

            def spread(column, name):
                everywhere = psum1.tile([P, P], F32, name=name, tag="spread", bufs=1)
                nc.tensor.matmul(out=everywhere[:], lhsT=column.to_broadcast([P, P]),
                                 rhs=identity_over_448[:], start=True, stop=True)
                return everywhere

            def scale_from(everywhere, max_over_448, scale):
                nc.vector.tensor_reduce(out=max_over_448[:], in_=everywhere[:], axis=AX.X, op=ALU.max)
                nc.vector.reciprocal(out=scale[:], in_=max_over_448[:])

            for n in range(TRANSPOSE_BANKS):
                transpose_x(n)

            clear_signs(0, 1, "vector", slice(0, K // 2))
            clear_signs(0, 1, "vector", slice(K // 2, K))
            max_of_x_unit(0)
            clear_signs(1, 2, "vector")
            max_of_x_unit(1)
            clear_signs(2, 3, "scalar")
            clear_signs(3, 4, "vector")
            max_of_x_unit(3)
            clear_signs(4, 5, "scalar")
            clear_signs(5, 6, "vector")
            max_of_x_unit(2)
            max_of_x_unit(5)
            clear_signs(6, 7, "scalar")
            clear_signs(7, 8, "vector")
            max_of_x_unit(4)
            max_of_x_unit(7)
            clear_signs(8, 10, "scalar")
            max_of_x_unit(6)
            nc.vector.tensor_reduce(out=x_part_max[:], in_=x_unit_max[:], axis=AX.X, op=ALU.max)
            x_everywhere = spread(x_part_max[:, 0:1], "x_everywhere")
            clear_signs(10, 12, "vector")
            scale_from(x_everywhere, x_max_over_448, xs)
            for n in range(ROW_TILES):
                scale_x(n)
            clear_signs(12, 14, "vector")
            max_of_w_units(8, 12)
            clear_signs(14, 16, "vector")
            clear_signs(16, 18, "vector")
            clear_signs(18, 20, "scalar")
            for n in range(ROW_TILES, 2 * ROW_TILES):
                scale_x(n)
            max_of_w_units(12, 16)
            clear_signs(20, 22, "vector")
            clear_signs(22, 24, "vector")
            max_of_w_units(16, 20)
            max_of_w_units(20, 24)
            w_everywhere = spread(w_part_max[:, W_MAXIMA - 1:W_MAXIMA], "w_everywhere")
            warm_up = psum1.tile([P, CHUNK], F32, name="warm_up", tag="bank")
            for d in range(WARM_UP_MATMULS):
                nc.tensor.matmul(out=warm_up[:], lhsT=w_sb[:, 0, 0:P], rhs=w_sb[:, 0, 0:CHUNK],
                                 start=True, stop=True)
            quantise_x(0, 0, ROW_TILES // 2)
            scale_from(w_everywhere, w_max_over_448, ws)

        w_by_row = w_sb[:].rearrange("p c (e n) -> p (c e) n", e=2)
        panels = {}

        def scale_w(j, g, engine):
            panel = slots.tile([P, PACK * CHUNK], BF16, name="panel", tag="slot", align_bytes=64)
            src = w_by_row[:, PACK * g:PACK * g + PACK, j * CHUNK:(j + 1) * CHUNK].rearrange(
                "p t (c i) -> p c t i", i=RUN)
            dst = panel[:].rearrange("p (c i t) -> p c t i", i=RUN, t=PACK)
            if engine == "vector":
                nc.vector.tensor_scalar(out=dst, in0=src, scalar1=ws[:, 0:1], scalar2=None,
                                        op0=ALU.mult)
            else:
                nc.scalar.activation(out=dst, in_=src, func=ACTF.Copy, scale=ws[:, 0:1])
            panels[(j, g)] = panel

        def quantise_w(j, g):
            b = (j * PASSES + g) * CHUNK
            nc.vector.quantize_mx(out=w_codes[:, b:b + CHUNK].bitcast(FP8X4), scales=w_scale_bytes[:, b:b + CHUNK],
                                  in_=panels[(j, g)][:])

        def mx_pass(acc, i, j, g, c0=0, c1=CHUNK):
            a = (g * ROW_TILES + i) * P
            b = (j * PASSES + g) * CHUNK
            nc.tensor.matmul_mx(out=acc[:], lhsT=x_codes[:, a:a + P].bitcast(FP8X4),
                                lhsT_scale=x_scale_bytes[:, a:a + P],
                                rhs=w_codes[:, b + c0:b + c1].bitcast(FP8X4),
                                rhs_scale=w_scale_bytes[:, b + c0:b + c1],
                                start=(g == 0), stop=(g == PASSES - 1))

        def finish(acc, i, j, engine, c0=0, c1=CHUNK):
            result = out_pool.tile([P, CHUNK], F32, name="result", tag="result")
            if engine == "vector":
                nc.vector.tensor_scalar(out=result[:, c0:c1], in0=acc[:], scalar1=out_factor[:, 0:1],
                                        scalar2=None, op0=ALU.mult)
            else:
                nc.scalar.activation(out=result[:, c0:c1], in_=acc[:], func=ACTF.Copy,
                                     scale=out_factor[:, 0:1])
            nc.sync.dma_start(out=out_rows[:, i, j * CHUNK + c0:j * CHUNK + c1], in_=result[:, c0:c1])

        with tc.psum_pool(name="psum2", bufs=ROW_TILES) as psum2:
            scale_w(0, 0, "vector")
            quantise_w(0, 0)
            scale_w(0, 1, "scalar")
            scale_w(0, 2, "scalar")
            scale_w(0, 3, "scalar")
            quantise_x(0, ROW_TILES // 2, ROW_TILES)
            for g in range(1, PASSES):
                quantise_x(g, 0, ROW_TILES)
                quantise_w(0, g)
            accs = {}
            for i in range(ROW_TILES):
                first_acc = psum2.tile([P, CHUNK], F32, name="acc", tag="acc")
                accs[i] = first_acc
            for g in range(PASSES):
                for i in range(ROW_TILES):
                    mx_pass(accs[i], i, 0, g)
            nc.vector.tensor_tensor(out=out_factor[:], in0=x_max_over_448[:], in1=w_max_over_448[:],
                                    op=ALU.mult)
            for j in range(1, CHUNKS):
                first_on_scalar = 2 if j == 1 else 3
                for g in range(first_on_scalar, PASSES):
                    scale_w(j, g, "scalar")
                for g in range(first_on_scalar):
                    scale_w(j, g, "vector")
                    if g > 0:
                        quantise_w(j, g - 1)
                for g in range(first_on_scalar - 1, PASSES):
                    quantise_w(j, g)
                for i in range(ROW_TILES):
                    finish(accs[i], i, j - 1, "scalar")
                for i in range(ROW_TILES if j < CHUNKS - 1 else ROW_TILES - 1):
                    acc = psum2.tile([P, CHUNK], F32, name="acc", tag="acc")
                    accs[i] = acc
                    for g in range(PASSES):
                        mx_pass(acc, i, j, g)
            for i in range(ROW_TILES - 1):
                finish(accs[i], i, CHUNKS - 1, "vector" if i % 2 else "scalar")
            for half in range(2):
                c0 = half * (CHUNK // 2)
                half_acc = psum2.tile([P, CHUNK // 2], F32, name="half_acc", tag="acc")
                for g in range(PASSES):
                    mx_pass(half_acc, ROW_TILES - 1, CHUNKS - 1, g, c0, c0 + CHUNK // 2)
                finish(half_acc, ROW_TILES - 1, CHUNKS - 1, "vector" if half == 0 else "scalar",
                       c0, c0 + CHUNK // 2)
